import numpy as np
import ml_dtypes


def mxq(x, axis, fmt="e4m3"):
    dtype, down = {"e4m3": (ml_dtypes.float8_e4m3fn, 7), "e5m2": (ml_dtypes.float8_e5m2, 14)}[fmt]
    v = np.moveaxis(np.asarray(x, np.float32).astype(ml_dtypes.bfloat16).astype(np.float64), axis, -1)
    blocks = v.reshape(v.shape[:-1] + (-1, 32))
    amax = np.abs(blocks).max(-1, keepdims=True)
    byte = np.maximum(np.where(amax > 0, np.frexp(amax)[1] - 1 + 127, 0) - down, 1)
    scale = np.exp2(byte - 127.0)
    codes = (blocks / scale).astype(np.float32).astype(dtype).astype(np.float64)
    return np.moveaxis((codes * scale).reshape(v.shape), -1, axis)


WIDE = False


def mx_kscale(k):
    if not WIDE:
        return np.ones(k)
    levels = np.array([10, -10, 5, -5, 0])
    a = np.random.permutation(np.resize(levels, k // 512 * 4)).reshape(k // 512, 4)
    idx = np.arange(k)
    return np.exp2(a[idx // 512, idx % 128 // 32])


BF16 = ml_dtypes.bfloat16


def bf(x):
    return np.asarray(x, np.float32).astype(BF16)


def f64(x):
    return np.asarray(x).astype(np.float64)


B, U, I, O = 128, 8, 512, 256


def sigmoid(v):
    return 1.0 / (1.0 + np.exp(-v))


def setup_inputs():
    s = mx_kscale(I)
    wi = lambda: bf(np.random.standard_normal((U, I, O)) / np.sqrt(I) / s[None, :, None])
    wh = lambda: bf(np.random.standard_normal((U, O, O)) / np.sqrt(O))
    return {"x": bf(np.random.standard_normal((B, U, I)) * s),
            "h": bf(np.random.standard_normal((B, U, O))),
            "w_ir": wi(), "w_iz": wi(), "w_in": wi(),
            "w_hr": wh(), "w_hz": wh(), "w_hn": wh()}


def reference(x, h, w_ir, w_iz, w_in, w_hr, w_hz, w_hn):
    xq = mxq(f64(x).transpose(1, 0, 2), 2, "e4m3")
    hu = f64(h).transpose(1, 0, 2)
    r = sigmoid((xq @ mxq(f64(w_ir), 1, "e4m3")) + hu @ f64(w_hr))
    z = sigmoid((xq @ mxq(f64(w_iz), 1, "e4m3")) + hu @ f64(w_hz))
    n = np.tanh((xq @ mxq(f64(w_in), 1, "e4m3")) + r * (hu @ f64(w_hn)))
    return ((1.0 - z) * n + z * hu).transpose(1, 0, 2)

@@ -1,0 +1,176 @@
+from contextlib import ExitStack
+
+import concourse.mybir as mybir
+from concourse.masks import make_identity
+
+BF16 = mybir.dt.bfloat16
+F32 = mybir.dt.float32
+U32 = mybir.dt.uint32
+U8 = mybir.dt.uint8
+FP8X4 = mybir.dt.float8_e4m3fn_x4
+ACT = mybir.ActivationFunctionType
+ALU = mybir.AluOpType
+
+P = 128
+UNITS = 8
+IN = 512
+HID = 256
+PACK = 4
+H_ROWS = HID // P
+GATES = 3
+R = 0
+Z = 1
+N = 2
+RUN = 4
+
+FLOPS = 2 * P * UNITS * GATES * (IN * HID + HID * HID)
+
+
+def tile_unitwisegru_pa_kernel(tc, x, h, w_ir, w_iz, w_in, w_hr, w_hz, w_hn, out):
+    nc = tc.nc
+    with ExitStack() as ctx:
+        keep = ctx.enter_context(tc.tile_pool(name="keep", bufs=1))
+        work = ctx.enter_context(tc.tile_pool(name="work", bufs=3))
+        psum_t = ctx.enter_context(tc.psum_pool(name="psum_t", bufs=2))
+        psum_g = ctx.enter_context(tc.psum_pool(name="psum_g", bufs=2))
+
+        x_sb = keep.tile([P, UNITS * IN], BF16)
+        h_sb = keep.tile([P, UNITS, HID], BF16)
+        wi_raw = [keep.tile([P, GATES, PACK, HID], BF16, name="wi_raw%d" % u) for u in range(UNITS)]
+        wh_sb = [keep.tile([P, GATES, H_ROWS, HID], BF16, name="wh_sb%d" % u) for u in range(UNITS)]
+
+        def load_input_weights(u):
+            for g, w in enumerate((w_ir, w_iz, w_in)):
+                nc.sync.dma_start(
+                    out=wi_raw[u][:, g], in_=w[u].rearrange("(p j) o -> p j o", j=PACK)
+                )
+
+        def load_hidden_weights(u):
+            for g, w in enumerate((w_hr, w_hz, w_hn)):
+                nc.sync.dma_start(
+                    out=wh_sb[u][:, g], in_=w[u].rearrange("(p c) o -> p c o", c=H_ROWS)
+                )
+
+        load_input_weights(0)
+        nc.sync.dma_start(out=x_sb[:], in_=x.rearrange("b u i -> b (u i)"))
+        nc.sync.dma_start(out=h_sb[:], in_=h)
+        load_hidden_weights(0)
+        for u in range(1, UNITS):
+            load_input_weights(u)
+            load_hidden_weights(u)
+
+        ident_f32 = keep.tile([P, P], F32)
+        make_identity(nc, ident_f32[:])
+        ident_bf16 = keep.tile([P, P], BF16)
+        make_identity(nc, ident_bf16[:])
+        warm = keep.tile([P, 1], F32)
+        nc.vector.memset(warm[:], 0.0)
+        nc.scalar.activation(out=warm[:], in_=warm[:], func=ACT.Sigmoid)
+
+        w_codes = [keep.tile([P, GATES * HID], U32, align_bytes=64, name="w_codes%d" % u) for u in range(UNITS)]
+        w_scales = [keep.tile([P, GATES * HID], U8, align_bytes=64, name="w_scales%d" % u) for u in range(UNITS)]
+
+        def quantise_weights(u):
+            grouped = work.tile([P, GATES, HID, PACK], BF16, align_bytes=64)
+            for g in range(GATES):
+                src = wi_raw[u][:, g].rearrange("p t (c i) -> p c t i", i=RUN)
+                dst = grouped[:, g].rearrange("p (c i) t -> p c t i", i=RUN)
+                if g == N:
+                    nc.vector.tensor_copy(out=dst, in_=src)
+                else:
+                    nc.scalar.copy(out=dst, in_=src)
+            for first, count in ((R, 2), (N, 1)):
+                cols = slice(first * HID, (first + count) * HID)
+                nc.vector.quantize_mx(
+                    out=w_codes[u][:, cols].bitcast(FP8X4),
+                    scales=w_scales[u][:, cols],
+                    in_=grouped[:, first : first + count].rearrange("p g o t -> p (g o t)"),
+                )
+
+        x_words = x_sb[:].bitcast(F32).rearrange("b (u p s) -> b u s p", u=UNITS, s=2)
+        x_grouped = keep.tile([P, UNITS * P * PACK], BF16, align_bytes=64)
+        x_grouped_words = x_grouped[:].bitcast(F32).rearrange("p (u b s) -> p u b s", u=UNITS, s=2)
+        x_codes = keep.tile([P, UNITS * P], U32, align_bytes=64)
+        x_scales = keep.tile([P, UNITS * P], U8, align_bytes=64)
+
+        def quantise_x(pair):
+            units = slice(2 * pair, 2 * pair + 2)
+            xt = psum_t.tile([P, 2, 2, P], F32, tag="transposed")
+            for i in range(2):
+                for s in range(2):
+                    nc.tensor.transpose(xt[:, i, s, :], x_words[:, 2 * pair + i, s, :], ident_f32[:])
+            halves_side_by_side = xt[:].rearrange("p i s b -> p i b s")
+            if pair % 2 == 0:
+                nc.vector.tensor_copy(out=x_grouped_words[:, units], in_=halves_side_by_side)
+            else:
+                nc.scalar.copy(out=x_grouped_words[:, units], in_=halves_side_by_side)
+            cols = slice(2 * pair * P, (2 * pair + 2) * P)
+            nc.vector.quantize_mx(
+                out=x_codes[:, cols].bitcast(FP8X4),
+                scales=x_scales[:, cols],
+                in_=x_grouped[:, 2 * pair * P * PACK : (2 * pair + 2) * P * PACK],
+            )
+
+        h_cols = h_sb[:].rearrange("b u (p c) -> b u c p", c=H_ROWS)
+        hT = keep.tile([P, UNITS, H_ROWS, P], BF16)
+
+        def transpose_h(half):
+            units = slice(4 * half, 4 * half + 4)
+            ht = psum_t.tile([P, 4, H_ROWS, P], BF16, tag="transposed")
+            for i in range(4):
+                for c in range(H_ROWS):
+                    nc.tensor.transpose(ht[:, i, c, :], h_cols[:, 4 * half + i, c, :], ident_bf16[:])
+            nc.scalar.copy(out=hT[:, units], in_=ht[:])
+
+        def gru_unit(u):
+            x_rz = psum_g.tile([P, 2 * HID], F32)
+            h_rz = psum_g.tile([P, 2, HID], F32)
+            xh_n = psum_g.tile([P, 2, HID], F32)
+            for acc, cols in ((x_rz[:], slice(0, 2 * HID)), (xh_n[:, 0, :], slice(2 * HID, 3 * HID))):
+                nc.tensor.matmul_mx(
+                    out=acc,
+                    lhsT=x_codes[:, u * P : (u + 1) * P].bitcast(FP8X4),
+                    lhsT_scale=x_scales[:, u * P : (u + 1) * P],
+                    rhs=w_codes[u][:, cols].bitcast(FP8X4),
+                    rhs_scale=w_scales[u][:, cols],
+                    start=True,
+                    stop=True,
+                )
+            for g, acc in ((R, h_rz[:, R, :]), (Z, h_rz[:, Z, :]), (N, xh_n[:, 1, :])):
+                for c in range(H_ROWS):
+                    nc.tensor.matmul(
+                        out=acc,
+                        lhsT=hT[:, u, c, :],
+                        rhs=wh_sb[u][:, g, c, :],
+                        start=(c == 0),
+                        stop=(c == H_ROWS - 1),
+                    )
+
+            h_rz_sb = work.tile([P, 2 * HID], F32)
+            nc.scalar.copy(out=h_rz_sb[:], in_=h_rz[:].rearrange("p g o -> p (g o)"))
+            rz_sum = work.tile([P, 2 * HID], F32)
+            nc.vector.tensor_tensor(out=rz_sum[:], in0=x_rz[:], in1=h_rz_sb[:], op=ALU.add)
+            rz = work.tile([P, 2, HID], F32)
+            nc.scalar.activation(out=rz[:].rearrange("p g o -> p (g o)"), in_=rz_sum[:], func=ACT.Sigmoid)
+
+            n_sum = work.tile([P, HID], F32)
+            nc.vector.tensor_tensor(out=n_sum[:], in0=xh_n[:, 1, :], in1=rz[:, R, :], op=ALU.mult)
+            nc.vector.tensor_tensor(out=n_sum[:], in0=xh_n[:, 0, :], in1=n_sum[:], op=ALU.add)
+            n_gate = work.tile([P, HID], F32)
+            nc.scalar.activation(out=n_gate[:], in_=n_sum[:], func=ACT.Tanh)
+
+            blend = work.tile([P, HID], F32)
+            nc.vector.tensor_tensor(out=blend[:], in0=h_sb[:, u, :], in1=n_gate[:], op=ALU.subtract)
+            nc.vector.tensor_tensor(out=blend[:], in0=blend[:], in1=rz[:, Z, :], op=ALU.mult)
+            nc.vector.tensor_tensor(out=blend[:], in0=blend[:], in1=n_gate[:], op=ALU.add)
+            nc.sync.dma_start(out=out[:, u, :], in_=blend[:])
+
+        quantise_weights(0)
+        for pair in range(UNITS // 2):
+            quantise_x(pair)
+        for half in range(2):
+            transpose_h(half)
+        for u in range(UNITS):
+            if u + 1 < UNITS:
+                quantise_weights(u + 1)
+            gru_unit(u)

@@ -13,6 +13,7 @@ ALU = mybir.AluOpType
 
 P = 128
 UNITS = 8
+PAIRS = UNITS // 2
 IN = 512
 HID = 256
 PACK = 4
@@ -28,149 +29,246 @@ FLOPS = 2 * P * UNITS * GATES * (IN * HID + HID * HID)
 
 def tile_unitwisegru_pa_kernel(tc, x, h, w_ir, w_iz, w_in, w_hr, w_hz, w_hn, out):
     nc = tc.nc
+    w_i = (w_ir, w_iz, w_in)
+    w_h = (w_hr, w_hz, w_hn)
+    RZ_COLS = slice(0, 2 * HID)
+    N_COLS = slice(2 * HID, 3 * HID)
     with ExitStack() as ctx:
         keep = ctx.enter_context(tc.tile_pool(name="keep", bufs=1))
         work = ctx.enter_context(tc.tile_pool(name="work", bufs=3))
         psum_t = ctx.enter_context(tc.psum_pool(name="psum_t", bufs=2))
         psum_g = ctx.enter_context(tc.psum_pool(name="psum_g", bufs=2))
+        ctx.enter_context(tc.manual_schedule())
 
-        x_sb = keep.tile([P, UNITS * IN], BF16)
-        h_sb = keep.tile([P, UNITS, HID], BF16)
+        x_sb = [keep.tile([P, 2 * IN], BF16, name="x_sb%d" % k) for k in range(PAIRS)]
+        h_sb = [keep.tile([P, 2, HID], BF16, name="h_sb%d" % k) for k in range(PAIRS)]
         wi_raw = [keep.tile([P, GATES, PACK, HID], BF16, name="wi_raw%d" % u) for u in range(UNITS)]
         wh_sb = [keep.tile([P, GATES, H_ROWS, HID], BF16, name="wh_sb%d" % u) for u in range(UNITS)]
 
+        def load_pair(k):
+            units = slice(2 * k, 2 * k + 2)
+            nc.sync.dma_start(out=h_sb[k][:], in_=h[:, units, :])
+            nc.sync.dma_start(out=x_sb[k][:], in_=x[:, units, :].rearrange("b u i -> b (u i)"))
+
         def load_input_weights(u):
-            for g, w in enumerate((w_ir, w_iz, w_in)):
+            for g in (R, Z, N):
                 nc.sync.dma_start(
-                    out=wi_raw[u][:, g], in_=w[u].rearrange("(p j) o -> p j o", j=PACK)
+                    out=wi_raw[u][:, g], in_=w_i[g][u].rearrange("(p j) o -> p j o", j=PACK)
                 )
 
         def load_hidden_weights(u):
-            for g, w in enumerate((w_hr, w_hz, w_hn)):
+            for g in (R, Z, N):
                 nc.sync.dma_start(
-                    out=wh_sb[u][:, g], in_=w[u].rearrange("(p c) o -> p c o", c=H_ROWS)
+                    out=wh_sb[u][:, g], in_=w_h[g][u].rearrange("(p c) o -> p c o", c=H_ROWS)
                 )
 
-        load_input_weights(0)
-        nc.sync.dma_start(out=x_sb[:], in_=x.rearrange("b u i -> b (u i)"))
-        nc.sync.dma_start(out=h_sb[:], in_=h)
-        load_hidden_weights(0)
-        for u in range(1, UNITS):
+        load_pair(0)
+        for u in range(UNITS):
             load_input_weights(u)
+            if u % 2 == 1 and u + 1 < UNITS:
+                load_pair((u + 1) // 2)
             load_hidden_weights(u)
 
-        ident_f32 = keep.tile([P, P], F32)
-        make_identity(nc, ident_f32[:])
         ident_bf16 = keep.tile([P, P], BF16)
         make_identity(nc, ident_bf16[:])
+        ident_f32 = keep.tile([P, P], F32)
+        make_identity(nc, ident_f32[:])
         warm = keep.tile([P, 1], F32)
         nc.vector.memset(warm[:], 0.0)
         nc.scalar.activation(out=warm[:], in_=warm[:], func=ACT.Sigmoid)
 
-        w_codes = [keep.tile([P, GATES * HID], U32, align_bytes=64, name="w_codes%d" % u) for u in range(UNITS)]
-        w_scales = [keep.tile([P, GATES * HID], U8, align_bytes=64, name="w_scales%d" % u) for u in range(UNITS)]
+        def is_unit(u):
+            return 0 <= u < UNITS
 
-        def quantise_weights(u):
-            grouped = work.tile([P, GATES, HID, PACK], BF16, align_bytes=64)
-            for g in range(GATES):
-                src = wi_raw[u][:, g].rearrange("p t (c i) -> p c t i", i=RUN)
-                dst = grouped[:, g].rearrange("p (c i) t -> p c t i", i=RUN)
-                if g == N:
-                    nc.vector.tensor_copy(out=dst, in_=src)
-                else:
-                    nc.scalar.copy(out=dst, in_=src)
-            for first, count in ((R, 2), (N, 1)):
-                cols = slice(first * HID, (first + count) * HID)
-                nc.vector.quantize_mx(
-                    out=w_codes[u][:, cols].bitcast(FP8X4),
-                    scales=w_scales[u][:, cols],
-                    in_=grouped[:, first : first + count].rearrange("p g o t -> p (g o t)"),
-                )
+        def is_pair(twice_k):
+            return twice_k % 2 == 0 and 0 <= twice_k // 2 < PAIRS
 
-        x_words = x_sb[:].bitcast(F32).rearrange("b (u p s) -> b u s p", u=UNITS, s=2)
-        x_grouped = keep.tile([P, UNITS * P * PACK], BF16, align_bytes=64)
-        x_grouped_words = x_grouped[:].bitcast(F32).rearrange("p (u b s) -> p u b s", u=UNITS, s=2)
-        x_codes = keep.tile([P, UNITS * P], U32, align_bytes=64)
-        x_scales = keep.tile([P, UNITS * P], U8, align_bytes=64)
+        transposed = {}
+        hT = [keep.tile([P, 2, H_ROWS, P], BF16, name="hT%d" % k) for k in range(PAIRS)]
+        x_grouped = {}
+        x_codes = [keep.tile([P, 2 * P], U32, align_bytes=64, name="x_codes%d" % k) for k in range(PAIRS)]
+        x_scales = [keep.tile([P, 2 * P], U8, align_bytes=64, name="x_scales%d" % k) for k in range(PAIRS)]
 
-        def quantise_x(pair):
-            units = slice(2 * pair, 2 * pair + 2)
+        def transpose_pair(twice_k):
+            if not is_pair(twice_k):
+                return
+            k = twice_k // 2
+            h_cols = h_sb[k][:].rearrange("b i (p c) -> b i c p", c=H_ROWS)
+            ht = psum_t.tile([P, 2, H_ROWS, P], BF16, tag="transposed")
+            for i in range(2):
+                for c in range(H_ROWS):
+                    nc.tensor.transpose(ht[:, i, c, :], h_cols[:, i, c, :], ident_bf16[:])
+            x_words = x_sb[k][:].bitcast(F32).rearrange("b (i p s) -> b i s p", i=2, s=2)
             xt = psum_t.tile([P, 2, 2, P], F32, tag="transposed")
             for i in range(2):
                 for s in range(2):
-                    nc.tensor.transpose(xt[:, i, s, :], x_words[:, 2 * pair + i, s, :], ident_f32[:])
-            halves_side_by_side = xt[:].rearrange("p i s b -> p i b s")
-            if pair % 2 == 0:
-                nc.vector.tensor_copy(out=x_grouped_words[:, units], in_=halves_side_by_side)
+                    nc.tensor.transpose(xt[:, i, s, :], x_words[:, i, s, :], ident_f32[:])
+            transposed[k] = (ht, xt)
+
+        def fetch_pair(twice_k):
+            if not is_pair(twice_k):
+                return
+            k = twice_k // 2
+            ht, xt = transposed[k]
+            nc.scalar.copy(out=hT[k][:], in_=ht[:])
+            x_grouped[k] = work.tile([P, 2 * P * PACK], BF16, align_bytes=64, name="x_grouped")
+            dst = x_grouped[k][:].bitcast(F32).rearrange("p (i b s) -> p i b s", i=2, s=2)
+            src = xt[:].rearrange("p i s b -> p i b s")
+            if k % 2 == 0:
+                nc.vector.tensor_copy(out=dst, in_=src)
             else:
-                nc.scalar.copy(out=x_grouped_words[:, units], in_=halves_side_by_side)
-            cols = slice(2 * pair * P, (2 * pair + 2) * P)
+                nc.scalar.copy(out=dst, in_=src)
+
+        def quantise_x(twice_k):
+            if not is_pair(twice_k):
+                return
+            k = twice_k // 2
             nc.vector.quantize_mx(
-                out=x_codes[:, cols].bitcast(FP8X4),
-                scales=x_scales[:, cols],
-                in_=x_grouped[:, 2 * pair * P * PACK : (2 * pair + 2) * P * PACK],
+                out=x_codes[k][:].bitcast(FP8X4), scales=x_scales[k][:], in_=x_grouped[k][:]
             )
 
-        h_cols = h_sb[:].rearrange("b u (p c) -> b u c p", c=H_ROWS)
-        hT = keep.tile([P, UNITS, H_ROWS, P], BF16)
+        grouped = {}
+        w_codes = [keep.tile([P, GATES * HID], U32, align_bytes=64, name="w_codes%d" % u) for u in range(UNITS)]
+        w_scales = [keep.tile([P, GATES * HID], U8, align_bytes=64, name="w_scales%d" % u) for u in range(UNITS)]
 
-        def transpose_h(half):
-            units = slice(4 * half, 4 * half + 4)
-            ht = psum_t.tile([P, 4, H_ROWS, P], BF16, tag="transposed")
-            for i in range(4):
-                for c in range(H_ROWS):
-                    nc.tensor.transpose(ht[:, i, c, :], h_cols[:, 4 * half + i, c, :], ident_bf16[:])
-            nc.scalar.copy(out=hT[:, units], in_=ht[:])
+        def regroup(u, g):
+            if not is_unit(u):
+                return
+            if u not in grouped:
+                grouped[u] = work.tile([P, GATES, HID, PACK], BF16, align_bytes=64, name="grouped")
+            src = wi_raw[u][:, g].rearrange("p t (c i) -> p c t i", i=RUN)
+            dst = grouped[u][:, g].rearrange("p (c i) t -> p c t i", i=RUN)
+            if g == N:
+                nc.vector.tensor_copy(out=dst, in_=src)
+            else:
+                nc.scalar.copy(out=dst, in_=src)
 
-        def gru_unit(u):
-            x_rz = psum_g.tile([P, 2 * HID], F32)
-            h_rz = psum_g.tile([P, 2, HID], F32)
-            xh_n = psum_g.tile([P, 2, HID], F32)
-            for acc, cols in ((x_rz[:], slice(0, 2 * HID)), (xh_n[:, 0, :], slice(2 * HID, 3 * HID))):
-                nc.tensor.matmul_mx(
+        def quantise(u, first, count, cols):
+            nc.vector.quantize_mx(
+                out=w_codes[u][:, cols].bitcast(FP8X4),
+                scales=w_scales[u][:, cols],
+                in_=grouped[u][:, first : first + count].rearrange("p g o t -> p (g o t)"),
+            )
+
+        def matmul_x(u, acc, cols):
+            b_cols = slice((u % 2) * P, (u % 2 + 1) * P)
+            nc.tensor.matmul_mx(
+                out=acc,
+                lhsT=x_codes[u // 2][:, b_cols].bitcast(FP8X4),
+                lhsT_scale=x_scales[u // 2][:, b_cols],
+                rhs=w_codes[u][:, cols].bitcast(FP8X4),
+                rhs_scale=w_scales[u][:, cols],
+                start=True,
+                stop=True,
+            )
+
+        def matmul_h(u, g, acc):
+            for c in range(H_ROWS):
+                nc.tensor.matmul(
                     out=acc,
-                    lhsT=x_codes[:, u * P : (u + 1) * P].bitcast(FP8X4),
-                    lhsT_scale=x_scales[:, u * P : (u + 1) * P],
-                    rhs=w_codes[u][:, cols].bitcast(FP8X4),
-                    rhs_scale=w_scales[u][:, cols],
-                    start=True,
-                    stop=True,
+                    lhsT=hT[u // 2][:, u % 2, c, :],
+                    rhs=wh_sb[u][:, g, c, :],
+                    start=(c == 0),
+                    stop=(c == H_ROWS - 1),
                 )
-            for g, acc in ((R, h_rz[:, R, :]), (Z, h_rz[:, Z, :]), (N, xh_n[:, 1, :])):
-                for c in range(H_ROWS):
-                    nc.tensor.matmul(
-                        out=acc,
-                        lhsT=hT[:, u, c, :],
-                        rhs=wh_sb[u][:, g, c, :],
-                        start=(c == 0),
-                        stop=(c == H_ROWS - 1),
-                    )
 
-            h_rz_sb = work.tile([P, 2 * HID], F32)
-            nc.scalar.copy(out=h_rz_sb[:], in_=h_rz[:].rearrange("p g o -> p (g o)"))
-            rz_sum = work.tile([P, 2 * HID], F32)
-            nc.vector.tensor_tensor(out=rz_sum[:], in0=x_rz[:], in1=h_rz_sb[:], op=ALU.add)
-            rz = work.tile([P, 2, HID], F32)
-            nc.scalar.activation(out=rz[:].rearrange("p g o -> p (g o)"), in_=rz_sum[:], func=ACT.Sigmoid)
+        x_rz = {}
+        h_rz = {}
+        xh_n = {}
+        h_rz_sb = {}
+        rz_sum = {}
+        rz = {}
+        rh_n = {}
+        n_sum = {}
+        z_h = {}
+        n_gate = {}
+        z_n = {}
 
-            n_sum = work.tile([P, HID], F32)
-            nc.vector.tensor_tensor(out=n_sum[:], in0=xh_n[:, 1, :], in1=rz[:, R, :], op=ALU.mult)
-            nc.vector.tensor_tensor(out=n_sum[:], in0=xh_n[:, 0, :], in1=n_sum[:], op=ALU.add)
-            n_gate = work.tile([P, HID], F32)
-            nc.scalar.activation(out=n_gate[:], in_=n_sum[:], func=ACT.Tanh)
+        def x_products_rz(u):
+            if not is_unit(u):
+                return
+            quantise(u, R, 2, RZ_COLS)
+            x_rz[u] = psum_g.tile([P, 2 * HID], F32, name="x_rz")
+            matmul_x(u, x_rz[u][:], RZ_COLS)
 
-            blend = work.tile([P, HID], F32)
-            nc.vector.tensor_tensor(out=blend[:], in0=h_sb[:, u, :], in1=n_gate[:], op=ALU.subtract)
-            nc.vector.tensor_tensor(out=blend[:], in0=blend[:], in1=rz[:, Z, :], op=ALU.mult)
-            nc.vector.tensor_tensor(out=blend[:], in0=blend[:], in1=n_gate[:], op=ALU.add)
-            nc.sync.dma_start(out=out[:, u, :], in_=blend[:])
+        def h_products_rz(u):
+            if not is_unit(u):
+                return
+            h_rz[u] = psum_g.tile([P, 2, HID], F32, name="h_rz")
+            matmul_h(u, R, h_rz[u][:, R, :])
+            matmul_h(u, Z, h_rz[u][:, Z, :])
+            h_rz_sb[u] = work.tile([P, 2 * HID], F32, name="h_rz_sb")
+            nc.scalar.copy(out=h_rz_sb[u][:], in_=h_rz[u][:].rearrange("p g o -> p (g o)"))
 
-        quantise_weights(0)
-        for pair in range(UNITS // 2):
-            quantise_x(pair)
-        for half in range(2):
-            transpose_h(half)
-        for u in range(UNITS):
-            if u + 1 < UNITS:
-                quantise_weights(u + 1)
-            gru_unit(u)
+        def h_product_n(u):
+            if not is_unit(u):
+                return
+            xh_n[u] = psum_g.tile([P, 2, HID], F32, name="xh_n")
+            matmul_h(u, N, xh_n[u][:, 1, :])
+
+        def x_product_n(u):
+            if not is_unit(u):
+                return
+            quantise(u, N, 1, N_COLS)
+            matmul_x(u, xh_n[u][:, 0, :], N_COLS)
+
+        def gates_rz(u):
+            if not is_unit(u):
+                return
+            rz_sum[u] = work.tile([P, 2 * HID], F32, name="rz_sum")
+            nc.vector.tensor_tensor(out=rz_sum[u][:], in0=x_rz[u][:], in1=h_rz_sb[u][:], op=ALU.add)
+            rz[u] = work.tile([P, 2, HID], F32, name="rz")
+            nc.scalar.activation(
+                out=rz[u][:].rearrange("p g o -> p (g o)"), in_=rz_sum[u][:], func=ACT.Sigmoid
+            )
+
+        def sum_n(u):
+            if not is_unit(u):
+                return
+            rh_n[u] = work.tile([P, HID], F32, name="rh_n")
+            nc.vector.tensor_tensor(out=rh_n[u][:], in0=xh_n[u][:, 1, :], in1=rz[u][:, R, :], op=ALU.mult)
+            z_h[u] = work.tile([P, HID], F32, name="z_h")
+            nc.vector.tensor_tensor(out=z_h[u][:], in0=h_sb[u // 2][:, u % 2, :], in1=rz[u][:, Z, :], op=ALU.mult)
+            n_sum[u] = work.tile([P, HID], F32, name="n_sum")
+            nc.vector.tensor_tensor(out=n_sum[u][:], in0=xh_n[u][:, 0, :], in1=rh_n[u][:], op=ALU.add)
+
+        def tanh_n(u):
+            if not is_unit(u):
+                return
+            n_gate[u] = work.tile([P, HID], F32, name="n_gate")
+            nc.scalar.activation(out=n_gate[u][:], in_=n_sum[u][:], func=ACT.Tanh)
+
+        def z_minus_1_times_n(u):
+            if not is_unit(u):
+                return
+            z_n[u] = work.tile([P, HID], F32, name="z_n")
+            nc.vector.scalar_tensor_tensor(
+                out=z_n[u][:], in0=rz[u][:, Z, :], scalar=1.0, in1=n_gate[u][:], op0=ALU.subtract, op1=ALU.mult
+            )
+
+        def blend_and_store(u):
+            if not is_unit(u):
+                return
+            result = work.tile([P, HID], F32)
+            nc.vector.tensor_tensor(out=result[:], in0=z_h[u][:], in1=z_n[u][:], op=ALU.subtract)
+            nc.sync.dma_start(out=out[:, u, :], in_=result[:])
+
+        def step(j):
+            x_products_rz(j + 1)
+            transpose_pair(j + 3)
+            sum_n(j)
+            z_minus_1_times_n(j - 1)
+            gates_rz(j + 1)
+            tanh_n(j)
+            h_products_rz(j + 2)
+            h_product_n(j + 1)
+            fetch_pair(j + 3)
+            regroup(j + 2, N)
+            blend_and_store(j - 1)
+            x_product_n(j + 1)
+            quantise_x(j + 2)
+            regroup(j + 3, R)
+            regroup(j + 3, Z)
+
+        for j in range(-3, UNITS + 1):
+            step(j)

@@ -249,7 +249,7 @@ def tile_unitwisegru_pa_kernel(tc, x, h, w_ir, w_iz, w_in, w_hr, w_hz, w_hn, out
         def blend_and_store(u):
             if not is_unit(u):
                 return
-            result = work.tile([P, HID], F32)
+            result = keep.tile([P, HID], F32, name="result%d" % u)
             nc.vector.tensor_tensor(out=result[:], in0=z_h[u][:], in1=z_n[u][:], op=ALU.subtract)
             nc.sync.dma_start(out=out[:, u, :], in_=result[:])
 

@@ -50,24 +50,28 @@ def tile_unitwisegru_pa_kernel(tc, x, h, w_ir, w_iz, w_in, w_hr, w_hz, w_hn, out
             nc.sync.dma_start(out=h_sb[k][:], in_=h[:, units, :])
             nc.sync.dma_start(out=x_sb[k][:], in_=x[:, units, :].rearrange("b u i -> b (u i)"))
 
-        def load_input_weights(u):
-            for g in (R, Z, N):
+        def load_input_weight(u, g):
+            if 0 <= u < UNITS:
                 nc.sync.dma_start(
                     out=wi_raw[u][:, g], in_=w_i[g][u].rearrange("(p j) o -> p j o", j=PACK)
                 )
 
-        def load_hidden_weights(u):
-            for g in (R, Z, N):
+        def load_hidden_weight(u, g):
+            if 0 <= u < UNITS:
                 nc.sync.dma_start(
                     out=wh_sb[u][:, g], in_=w_h[g][u].rearrange("(p c) o -> p c o", c=H_ROWS)
                 )
 
         load_pair(0)
-        for u in range(UNITS):
-            load_input_weights(u)
+        for u in range(UNITS + 1):
+            load_input_weight(u, R)
+            load_input_weight(u, Z)
             if u % 2 == 1 and u + 1 < UNITS:
                 load_pair((u + 1) // 2)
-            load_hidden_weights(u)
+            load_hidden_weight(u, R)
+            load_hidden_weight(u, Z)
+            load_hidden_weight(u - 1, N)
+            load_input_weight(u, N)
 
         ident_bf16 = keep.tile([P, P], BF16)
         make_identity(nc, ident_bf16[:])
@@ -114,7 +118,7 @@ def tile_unitwisegru_pa_kernel(tc, x, h, w_ir, w_iz, w_in, w_hr, w_hz, w_hn, out
             x_grouped[k] = work.tile([P, 2 * P * PACK], BF16, align_bytes=64, name="x_grouped")
             dst = x_grouped[k][:].bitcast(F32).rearrange("p (i b s) -> p i b s", i=2, s=2)
             src = xt[:].rearrange("p i s b -> p i b s")
-            if k % 2 == 0:
+            if k < PAIRS // 2:
                 nc.vector.tensor_copy(out=dst, in_=src)
             else:
                 nc.scalar.copy(out=dst, in_=src)

@@ -23,6 +23,7 @@ R = 0
 Z = 1
 N = 2
 RUN = 4
+UNITS_WITH_Z_ON_VECTOR = 4
 
 FLOPS = 2 * P * UNITS * GATES * (IN * HID + HID * HID)
 
@@ -109,19 +110,18 @@ def tile_unitwisegru_pa_kernel(tc, x, h, w_ir, w_iz, w_in, w_hr, w_hz, w_hn, out
                     nc.tensor.transpose(xt[:, i, s, :], x_words[:, i, s, :], ident_f32[:])
             transposed[k] = (ht, xt)
 
-        def fetch_pair(twice_k):
+        def fetch_h(twice_k):
+            if is_pair(twice_k):
+                k = twice_k // 2
+                nc.scalar.copy(out=hT[k][:], in_=transposed[k][0][:])
+
+        def fetch_x(twice_k):
             if not is_pair(twice_k):
                 return
             k = twice_k // 2
-            ht, xt = transposed[k]
-            nc.scalar.copy(out=hT[k][:], in_=ht[:])
             x_grouped[k] = work.tile([P, 2 * P * PACK], BF16, align_bytes=64, name="x_grouped")
             dst = x_grouped[k][:].bitcast(F32).rearrange("p (i b s) -> p i b s", i=2, s=2)
-            src = xt[:].rearrange("p i s b -> p i b s")
-            if k < PAIRS // 2:
-                nc.vector.tensor_copy(out=dst, in_=src)
-            else:
-                nc.scalar.copy(out=dst, in_=src)
+            nc.scalar.copy(out=dst, in_=transposed[k][1][:].rearrange("p i s b -> p i b s"))
 
         def quantise_x(twice_k):
             if not is_pair(twice_k):
@@ -131,28 +131,43 @@ def tile_unitwisegru_pa_kernel(tc, x, h, w_ir, w_iz, w_in, w_hr, w_hz, w_hn, out
                 out=x_codes[k][:].bitcast(FP8X4), scales=x_scales[k][:], in_=x_grouped[k][:]
             )
 
-        grouped = {}
+        grouped_rz = {}
+        grouped_n = {}
         w_codes = [keep.tile([P, GATES * HID], U32, align_bytes=64, name="w_codes%d" % u) for u in range(UNITS)]
         w_scales = [keep.tile([P, GATES * HID], U8, align_bytes=64, name="w_scales%d" % u) for u in range(UNITS)]
 
         def regroup(u, g):
             if not is_unit(u):
                 return
-            if u not in grouped:
-                grouped[u] = work.tile([P, GATES, HID, PACK], BF16, align_bytes=64, name="grouped")
-            src = wi_raw[u][:, g].rearrange("p t (c i) -> p c t i", i=RUN)
-            dst = grouped[u][:, g].rearrange("p (c i) t -> p c t i", i=RUN)
             if g == N:
+                grouped_n[u] = work.tile([P, HID, PACK], BF16, align_bytes=64, name="grouped_n")
+                whole = grouped_n[u][:]
+            else:
+                if u not in grouped_rz:
+                    grouped_rz[u] = work.tile([P, 2, HID, PACK], BF16, align_bytes=64, name="grouped_rz")
+                whole = grouped_rz[u][:, g]
+            src = wi_raw[u][:, g].rearrange("p t (c i) -> p c t i", i=RUN)
+            dst = whole.rearrange("p (c i) t -> p c t i", i=RUN)
+            if (g == N and u < UNITS - 1) or (g == Z and u < UNITS_WITH_Z_ON_VECTOR):
                 nc.vector.tensor_copy(out=dst, in_=src)
             else:
                 nc.scalar.copy(out=dst, in_=src)
 
-        def quantise(u, first, count, cols):
-            nc.vector.quantize_mx(
-                out=w_codes[u][:, cols].bitcast(FP8X4),
-                scales=w_scales[u][:, cols],
-                in_=grouped[u][:, first : first + count].rearrange("p g o t -> p (g o t)"),
-            )
+        def quantise_rz(u):
+            if is_unit(u):
+                nc.vector.quantize_mx(
+                    out=w_codes[u][:, RZ_COLS].bitcast(FP8X4),
+                    scales=w_scales[u][:, RZ_COLS],
+                    in_=grouped_rz[u][:].rearrange("p g o t -> p (g o t)"),
+                )
+
+        def quantise_n(u):
+            if is_unit(u):
+                nc.vector.quantize_mx(
+                    out=w_codes[u][:, N_COLS].bitcast(FP8X4),
+                    scales=w_scales[u][:, N_COLS],
+                    in_=grouped_n[u][:].rearrange("p o t -> p (o t)"),
+                )
 
         def matmul_x(u, acc, cols):
             b_cols = slice((u % 2) * P, (u % 2 + 1) * P)
@@ -189,52 +204,56 @@ def tile_unitwisegru_pa_kernel(tc, x, h, w_ir, w_iz, w_in, w_hr, w_hz, w_hn, out
         z_n = {}
 
         def x_products_rz(u):
-            if not is_unit(u):
-                return
-            quantise(u, R, 2, RZ_COLS)
-            x_rz[u] = psum_g.tile([P, 2 * HID], F32, name="x_rz")
-            matmul_x(u, x_rz[u][:], RZ_COLS)
+            if is_unit(u):
+                x_rz[u] = psum_g.tile([P, 2 * HID], F32, name="x_rz")
+                matmul_x(u, x_rz[u][:], RZ_COLS)
 
         def h_products_rz(u):
-            if not is_unit(u):
-                return
-            h_rz[u] = psum_g.tile([P, 2, HID], F32, name="h_rz")
-            matmul_h(u, R, h_rz[u][:, R, :])
-            matmul_h(u, Z, h_rz[u][:, Z, :])
-            h_rz_sb[u] = work.tile([P, 2 * HID], F32, name="h_rz_sb")
-            nc.scalar.copy(out=h_rz_sb[u][:], in_=h_rz[u][:].rearrange("p g o -> p (g o)"))
+            if is_unit(u):
+                h_rz[u] = psum_g.tile([P, 2, HID], F32, name="h_rz")
+                matmul_h(u, R, h_rz[u][:, R, :])
+                matmul_h(u, Z, h_rz[u][:, Z, :])
+
+        def fetch_h_rz(u):
+            if is_unit(u):
+                h_rz_sb[u] = work.tile([P, 2 * HID], F32, name="h_rz_sb")
+                nc.scalar.copy(out=h_rz_sb[u][:], in_=h_rz[u][:].rearrange("p g o -> p (g o)"))
 
         def h_product_n(u):
-            if not is_unit(u):
-                return
-            xh_n[u] = psum_g.tile([P, 2, HID], F32, name="xh_n")
-            matmul_h(u, N, xh_n[u][:, 1, :])
+            if is_unit(u):
+                xh_n[u] = psum_g.tile([P, 2, HID], F32, name="xh_n")
+                matmul_h(u, N, xh_n[u][:, 1, :])
 
         def x_product_n(u):
-            if not is_unit(u):
-                return
-            quantise(u, N, 1, N_COLS)
-            matmul_x(u, xh_n[u][:, 0, :], N_COLS)
+            if is_unit(u):
+                matmul_x(u, xh_n[u][:, 0, :], N_COLS)
 
-        def gates_rz(u):
-            if not is_unit(u):
-                return
-            rz_sum[u] = work.tile([P, 2 * HID], F32, name="rz_sum")
-            nc.vector.tensor_tensor(out=rz_sum[u][:], in0=x_rz[u][:], in1=h_rz_sb[u][:], op=ALU.add)
-            rz[u] = work.tile([P, 2, HID], F32, name="rz")
-            nc.scalar.activation(
-                out=rz[u][:].rearrange("p g o -> p (g o)"), in_=rz_sum[u][:], func=ACT.Sigmoid
-            )
+        def sum_rz(u):
+            if is_unit(u):
+                rz_sum[u] = work.tile([P, 2 * HID], F32, name="rz_sum")
+                nc.vector.tensor_tensor(out=rz_sum[u][:], in0=x_rz[u][:], in1=h_rz_sb[u][:], op=ALU.add)
+
+        def sigmoid_rz(u):
+            if is_unit(u):
+                rz[u] = work.tile([P, 2, HID], F32, name="rz")
+                nc.scalar.activation(
+                    out=rz[u][:].rearrange("p g o -> p (g o)"), in_=rz_sum[u][:], func=ACT.Sigmoid
+                )
+
+        def r_times_h_n(u):
+            if is_unit(u):
+                rh_n[u] = work.tile([P, HID], F32, name="rh_n")
+                nc.vector.tensor_tensor(out=rh_n[u][:], in0=xh_n[u][:, 1, :], in1=rz[u][:, R, :], op=ALU.mult)
+
+        def z_times_h(u):
+            if is_unit(u):
+                z_h[u] = work.tile([P, HID], F32, name="z_h")
+                nc.vector.tensor_tensor(out=z_h[u][:], in0=h_sb[u // 2][:, u % 2, :], in1=rz[u][:, Z, :], op=ALU.mult)
 
         def sum_n(u):
-            if not is_unit(u):
-                return
-            rh_n[u] = work.tile([P, HID], F32, name="rh_n")
-            nc.vector.tensor_tensor(out=rh_n[u][:], in0=xh_n[u][:, 1, :], in1=rz[u][:, R, :], op=ALU.mult)
-            z_h[u] = work.tile([P, HID], F32, name="z_h")
-            nc.vector.tensor_tensor(out=z_h[u][:], in0=h_sb[u // 2][:, u % 2, :], in1=rz[u][:, Z, :], op=ALU.mult)
-            n_sum[u] = work.tile([P, HID], F32, name="n_sum")
-            nc.vector.tensor_tensor(out=n_sum[u][:], in0=xh_n[u][:, 0, :], in1=rh_n[u][:], op=ALU.add)
+            if is_unit(u):
+                n_sum[u] = work.tile([P, HID], F32, name="n_sum")
+                nc.vector.tensor_tensor(out=n_sum[u][:], in0=xh_n[u][:, 0, :], in1=rh_n[u][:], op=ALU.add)
 
         def tanh_n(u):
             if not is_unit(u):
@@ -258,21 +277,31 @@ def tile_unitwisegru_pa_kernel(tc, x, h, w_ir, w_iz, w_in, w_hr, w_hz, w_hn, out
             nc.sync.dma_start(out=out[:, u, :], in_=result[:])
 
         def step(j):
-            x_products_rz(j + 1)
-            transpose_pair(j + 3)
-            sum_n(j)
-            z_minus_1_times_n(j - 1)
-            gates_rz(j + 1)
-            tanh_n(j)
-            h_products_rz(j + 2)
-            h_product_n(j + 1)
-            fetch_pair(j + 3)
-            regroup(j + 2, N)
-            blend_and_store(j - 1)
-            x_product_n(j + 1)
-            quantise_x(j + 2)
             regroup(j + 3, R)
-            regroup(j + 3, Z)
+            transpose_pair(j + 4)
+            h_products_rz(j + 3)
+            r_times_h_n(j)
+            sum_rz(j + 1)
+            if j + 3 >= UNITS_WITH_Z_ON_VECTOR:
+                regroup(j + 3, Z)
+            fetch_h(j + 4)
+            sigmoid_rz(j + 1)
+            sum_n(j)
+            fetch_x(j + 4)
+            tanh_n(j)
+            fetch_h_rz(j + 3)
+            quantise_x(j + 2)
+            h_product_n(j + 1)
+            x_product_n(j + 1)
+            x_products_rz(j + 2)
+            z_minus_1_times_n(j - 1)
+            z_times_h(j)
+            blend_and_store(j - 1)
+            if j + 3 < UNITS_WITH_Z_ON_VECTOR:
+                regroup(j + 3, Z)
+            quantise_n(j + 2)
+            regroup(j + 3, N)
+            quantise_rz(j + 3)
 
-        for j in range(-3, UNITS + 1):
+        for j in range(-4, UNITS + 1):
             step(j)

@@ -228,22 +228,33 @@ def tile_unitwisegru_pa_kernel(tc, x, h, w_ir, w_iz, w_in, w_hr, w_hz, w_hn, out
             if is_unit(u):
                 matmul_x(u, xh_n[u][:, 0, :], N_COLS)
 
+        def column_parts(u):
+            if u == UNITS - 1:
+                return (slice(0, HID // 2), slice(HID // 2, HID))
+            return (slice(0, HID),)
+
         def sum_rz(u):
             if is_unit(u):
-                rz_sum[u] = work.tile([P, 2 * HID], F32, name="rz_sum")
-                nc.vector.tensor_tensor(out=rz_sum[u][:], in0=x_rz[u][:], in1=h_rz_sb[u][:], op=ALU.add)
+                rz_sum[u] = work.tile([P, 2, HID], F32, name="rz_sum")
+                for cols in column_parts(u):
+                    nc.vector.tensor_tensor(
+                        out=rz_sum[u][:, :, cols],
+                        in0=x_rz[u][:].rearrange("p (g o) -> p g o", g=2)[:, :, cols],
+                        in1=h_rz_sb[u][:].rearrange("p (g o) -> p g o", g=2)[:, :, cols],
+                        op=ALU.add,
+                    )
 
         def sigmoid_rz(u):
             if is_unit(u):
                 rz[u] = work.tile([P, 2, HID], F32, name="rz")
-                nc.scalar.activation(
-                    out=rz[u][:].rearrange("p g o -> p (g o)"), in_=rz_sum[u][:], func=ACT.Sigmoid
-                )
+                for cols in column_parts(u):
+                    nc.scalar.activation(out=rz[u][:, :, cols], in_=rz_sum[u][:, :, cols], func=ACT.Sigmoid)
 
         def r_times_h_n(u):
             if is_unit(u):
                 rh_n[u] = work.tile([P, HID], F32, name="rh_n")
-                nc.vector.tensor_tensor(out=rh_n[u][:], in0=xh_n[u][:, 1, :], in1=rz[u][:, R, :], op=ALU.mult)
+                for cols in column_parts(u):
+                    nc.vector.tensor_tensor(out=rh_n[u][:, cols], in0=xh_n[u][:, 1, cols], in1=rz[u][:, R, cols], op=ALU.mult)
 
         def z_times_h(u):
             if is_unit(u):
@@ -253,21 +264,24 @@ def tile_unitwisegru_pa_kernel(tc, x, h, w_ir, w_iz, w_in, w_hr, w_hz, w_hn, out
         def sum_n(u):
             if is_unit(u):
                 n_sum[u] = work.tile([P, HID], F32, name="n_sum")
-                nc.vector.tensor_tensor(out=n_sum[u][:], in0=xh_n[u][:, 0, :], in1=rh_n[u][:], op=ALU.add)
+                for cols in column_parts(u):
+                    nc.vector.tensor_tensor(out=n_sum[u][:, cols], in0=xh_n[u][:, 0, cols], in1=rh_n[u][:, cols], op=ALU.add)
 
         def tanh_n(u):
             if not is_unit(u):
                 return
             n_gate[u] = work.tile([P, HID], F32, name="n_gate")
-            nc.scalar.activation(out=n_gate[u][:], in_=n_sum[u][:], func=ACT.Tanh)
+            for cols in column_parts(u):
+                nc.scalar.activation(out=n_gate[u][:, cols], in_=n_sum[u][:, cols], func=ACT.Tanh)
 
         def z_minus_1_times_n(u):
             if not is_unit(u):
                 return
             z_n[u] = work.tile([P, HID], F32, name="z_n")
-            nc.vector.scalar_tensor_tensor(
-                out=z_n[u][:], in0=rz[u][:, Z, :], scalar=1.0, in1=n_gate[u][:], op0=ALU.subtract, op1=ALU.mult
-            )
+            for cols in column_parts(u):
+                nc.vector.scalar_tensor_tensor(
+                    out=z_n[u][:, cols], in0=rz[u][:, Z, cols], scalar=1.0, in1=n_gate[u][:, cols], op0=ALU.subtract, op1=ALU.mult
+                )
 
         def blend_and_store(u):
             if not is_unit(u):

@@ -63,16 +63,15 @@ def tile_unitwisegru_pa_kernel(tc, x, h, w_ir, w_iz, w_in, w_hr, w_hz, w_hn, out
                     out=wh_sb[u][:, g], in_=w_h[g][u].rearrange("(p c) o -> p c o", c=H_ROWS)
                 )
 
-        load_pair(0)
-        for u in range(UNITS + 1):
+        for u in range(UNITS + 2):
             load_input_weight(u, R)
-            load_input_weight(u, Z)
-            if u % 2 == 1 and u + 1 < UNITS:
-                load_pair((u + 1) // 2)
-            load_hidden_weight(u, R)
-            load_hidden_weight(u, Z)
-            load_hidden_weight(u - 1, N)
             load_input_weight(u, N)
+            if u % 2 == 0 and u < UNITS:
+                load_pair(u // 2)
+            load_input_weight(u, Z)
+            load_hidden_weight(u - 1, Z)
+            load_hidden_weight(u - 1, R)
+            load_hidden_weight(u - 2, N)
 
         ident_bf16 = keep.tile([P, P], BF16)
         make_identity(nc, ident_bf16[:])
@@ -136,6 +135,9 @@ def tile_unitwisegru_pa_kernel(tc, x, h, w_ir, w_iz, w_in, w_hr, w_hz, w_hn, out
         w_codes = [keep.tile([P, GATES * HID], U32, align_bytes=64, name="w_codes%d" % u) for u in range(UNITS)]
         w_scales = [keep.tile([P, GATES * HID], U8, align_bytes=64, name="w_scales%d" % u) for u in range(UNITS)]
 
+        def z_on_vector(u):
+            return u in (0,1,2,4,6)
+
         def regroup(u, g):
             if not is_unit(u):
                 return
@@ -148,7 +150,7 @@ def tile_unitwisegru_pa_kernel(tc, x, h, w_ir, w_iz, w_in, w_hr, w_hz, w_hn, out
                 whole = grouped_rz[u][:, g]
             src = wi_raw[u][:, g].rearrange("p t (c i) -> p c t i", i=RUN)
             dst = whole.rearrange("p (c i) t -> p c t i", i=RUN)
-            if (g == N and u < UNITS - 1) or (g == Z and u < UNITS_WITH_Z_ON_VECTOR):
+            if g == N or (g == Z and z_on_vector(u)):
                 nc.vector.tensor_copy(out=dst, in_=src)
             else:
                 nc.scalar.copy(out=dst, in_=src)
@@ -181,22 +183,24 @@ def tile_unitwisegru_pa_kernel(tc, x, h, w_ir, w_iz, w_in, w_hr, w_hz, w_hn, out
                 stop=True,
             )
 
-        def matmul_h(u, g, acc):
+        def matmul_h(u, g, acc, stop=True):
             for c in range(H_ROWS):
                 nc.tensor.matmul(
                     out=acc,
                     lhsT=hT[u // 2][:, u % 2, c, :],
                     rhs=wh_sb[u][:, g, c, :],
                     start=(c == 0),
-                    stop=(c == H_ROWS - 1),
+                    stop=(stop and c == H_ROWS - 1),
                 )
 
         x_rz = {}
-        h_rz = {}
+        x_rz_sb = {}
+        h_r = {}
+        z_sum = {}
         xh_n = {}
-        h_rz_sb = {}
-        rz_sum = {}
-        rz = {}
+        r_sum = {}
+        r = {}
+        z = {}
         rh_n = {}
         n_sum = {}
         z_h = {}
@@ -205,19 +209,29 @@ def tile_unitwisegru_pa_kernel(tc, x, h, w_ir, w_iz, w_in, w_hr, w_hz, w_hn, out
 
         def x_products_rz(u):
             if is_unit(u):
-                x_rz[u] = psum_g.tile([P, 2 * HID], F32, name="x_rz")
+                x_rz[u] = psum_g.tile([P, 2 * HID], F32, name="x_rz", bufs=1)
                 matmul_x(u, x_rz[u][:], RZ_COLS)
 
-        def h_products_rz(u):
+        def fetch_x_rz(u):
             if is_unit(u):
-                h_rz[u] = psum_g.tile([P, 2, HID], F32, name="h_rz")
-                matmul_h(u, R, h_rz[u][:, R, :])
-                matmul_h(u, Z, h_rz[u][:, Z, :])
+                x_rz_sb[u] = work.tile([P, 2, HID], F32, name="x_rz_sb")
+                nc.scalar.copy(out=x_rz_sb[u][:], in_=x_rz[u][:].rearrange("p (g o) -> p g o", g=2))
 
-        def fetch_h_rz(u):
+        def h_product_r(u):
             if is_unit(u):
-                h_rz_sb[u] = work.tile([P, 2 * HID], F32, name="h_rz_sb")
-                nc.scalar.copy(out=h_rz_sb[u][:], in_=h_rz[u][:].rearrange("p g o -> p (g o)"))
+                h_r[u] = psum_g.tile([P, HID], F32, name="h_r", bufs=1)
+                matmul_h(u, R, h_r[u][:])
+
+        def h_product_z(u):
+            if is_unit(u):
+                z_sum[u] = psum_g.tile([P, HID], F32, name="z_sum")
+                matmul_h(u, Z, z_sum[u][:], stop=False)
+
+        def add_x_z(u):
+            if is_unit(u):
+                nc.tensor.matmul(
+                    out=z_sum[u][:], lhsT=ident_f32[:], rhs=x_rz_sb[u][:, Z, :], start=False, stop=True
+                )
 
         def h_product_n(u):
             if is_unit(u):
@@ -233,33 +247,33 @@ def tile_unitwisegru_pa_kernel(tc, x, h, w_ir, w_iz, w_in, w_hr, w_hz, w_hn, out
                 return (slice(0, HID // 2), slice(HID // 2, HID))
             return (slice(0, HID),)
 
-        def sum_rz(u):
+        def sum_r(u):
             if is_unit(u):
-                rz_sum[u] = work.tile([P, 2, HID], F32, name="rz_sum")
+                r_sum[u] = work.tile([P, HID], F32, name="r_sum")
                 for cols in column_parts(u):
-                    nc.vector.tensor_tensor(
-                        out=rz_sum[u][:, :, cols],
-                        in0=x_rz[u][:].rearrange("p (g o) -> p g o", g=2)[:, :, cols],
-                        in1=h_rz_sb[u][:].rearrange("p (g o) -> p g o", g=2)[:, :, cols],
-                        op=ALU.add,
-                    )
+                    nc.vector.tensor_tensor(out=r_sum[u][:, cols], in0=h_r[u][:, cols], in1=x_rz_sb[u][:, R, cols], op=ALU.add)
 
-        def sigmoid_rz(u):
+        def sigmoid_r(u):
             if is_unit(u):
-                rz[u] = work.tile([P, 2, HID], F32, name="rz")
+                r[u] = work.tile([P, HID], F32, name="r")
                 for cols in column_parts(u):
-                    nc.scalar.activation(out=rz[u][:, :, cols], in_=rz_sum[u][:, :, cols], func=ACT.Sigmoid)
+                    nc.scalar.activation(out=r[u][:, cols], in_=r_sum[u][:, cols], func=ACT.Sigmoid)
+
+        def sigmoid_z(u):
+            if is_unit(u):
+                z[u] = work.tile([P, HID], F32, name="z")
+                nc.scalar.activation(out=z[u][:], in_=z_sum[u][:], func=ACT.Sigmoid)
 
         def r_times_h_n(u):
             if is_unit(u):
                 rh_n[u] = work.tile([P, HID], F32, name="rh_n")
                 for cols in column_parts(u):
-                    nc.vector.tensor_tensor(out=rh_n[u][:, cols], in0=xh_n[u][:, 1, cols], in1=rz[u][:, R, cols], op=ALU.mult)
+                    nc.vector.tensor_tensor(out=rh_n[u][:, cols], in0=xh_n[u][:, 1, cols], in1=r[u][:, cols], op=ALU.mult)
 
         def z_times_h(u):
             if is_unit(u):
                 z_h[u] = work.tile([P, HID], F32, name="z_h")
-                nc.vector.tensor_tensor(out=z_h[u][:], in0=h_sb[u // 2][:, u % 2, :], in1=rz[u][:, Z, :], op=ALU.mult)
+                nc.vector.tensor_tensor(out=z_h[u][:], in0=h_sb[u // 2][:, u % 2, :], in1=z[u][:], op=ALU.mult)
 
         def sum_n(u):
             if is_unit(u):
@@ -280,7 +294,7 @@ def tile_unitwisegru_pa_kernel(tc, x, h, w_ir, w_iz, w_in, w_hr, w_hz, w_hn, out
             z_n[u] = work.tile([P, HID], F32, name="z_n")
             for cols in column_parts(u):
                 nc.vector.scalar_tensor_tensor(
-                    out=z_n[u][:, cols], in0=rz[u][:, Z, cols], scalar=1.0, in1=n_gate[u][:, cols], op0=ALU.subtract, op1=ALU.mult
+                    out=z_n[u][:, cols], in0=z[u][:, cols], scalar=1.0, in1=n_gate[u][:, cols], op0=ALU.subtract, op1=ALU.mult
                 )
 
         def blend_and_store(u):
@@ -290,32 +304,70 @@ def tile_unitwisegru_pa_kernel(tc, x, h, w_ir, w_iz, w_in, w_hr, w_hz, w_hn, out
             nc.vector.tensor_tensor(out=result[:], in0=z_h[u][:], in1=z_n[u][:], op=ALU.subtract)
             nc.sync.dma_start(out=out[:, u, :], in_=result[:])
 
-        def step(j):
-            regroup(j + 3, R)
-            transpose_pair(j + 4)
-            h_products_rz(j + 3)
-            r_times_h_n(j)
-            sum_rz(j + 1)
-            if j + 3 >= UNITS_WITH_Z_ON_VECTOR:
-                regroup(j + 3, Z)
-            fetch_h(j + 4)
-            sigmoid_rz(j + 1)
-            sum_n(j)
-            fetch_x(j + 4)
-            tanh_n(j)
-            fetch_h_rz(j + 3)
-            quantise_x(j + 2)
-            h_product_n(j + 1)
-            x_product_n(j + 1)
-            x_products_rz(j + 2)
-            z_minus_1_times_n(j - 1)
-            z_times_h(j)
-            blend_and_store(j - 1)
-            if j + 3 < UNITS_WITH_Z_ON_VECTOR:
-                regroup(j + 3, Z)
-            quantise_n(j + 2)
-            regroup(j + 3, N)
-            quantise_rz(j + 3)
+        def step(a):
+            regroup(a, R)
+            r_times_h_n(a - 3)
+            sigmoid_z(a - 2)
+            quantise_n(a - 1)
+            sum_n(a - 3)
+            tanh_n(a - 3)
+            quantise_x(a - 1)
+            quantise_rz(a - 1)
+            x_products_rz(a - 1)
+            h_product_z(a - 1)
+            sum_r(a - 2)
+            sigmoid_r(a - 2)
+            h_product_r(a - 1)
+            h_product_n(a - 2)
+            x_product_n(a - 2)
+            regroup(a, N)
+            z_minus_1_times_n(a - 3)
+            fetch_h(a)
+            fetch_x(a)
+            fetch_x_rz(a - 1)
+            add_x_z(a - 1)
+            if not z_on_vector(a):
+                regroup(a, Z)
+            transpose_pair(a + 1)
+            if z_on_vector(a):
+                regroup(a, Z)
+            z_times_h(a - 2)
+            blend_and_store(a - 3)
 
-        for j in range(-4, UNITS + 1):
-            step(j)
+        for a in range(-1, UNITS):
+            step(a)
+        y, z_ = UNITS - 2, UNITS - 1
+        h_product_z(z_)
+        r_times_h_n(y - 1)
+        sigmoid_z(y)
+        quantise_n(z_)
+        sum_n(y - 1)
+        tanh_n(y - 1)
+        quantise_rz(z_)
+        x_products_rz(z_)
+        sum_r(y)
+        sigmoid_r(y)
+        h_product_r(z_)
+        h_product_n(y)
+        x_product_n(y)
+        h_product_n(z_)
+        x_product_n(z_)
+        fetch_x_rz(z_)
+        add_x_z(z_)
+        z_times_h(y)
+        z_minus_1_times_n(y - 1)
+        blend_and_store(y - 1)
+        r_times_h_n(y)
+        sum_r(z_)
+        sigmoid_r(z_)
+        sum_n(y)
+        sigmoid_z(z_)
+        tanh_n(y)
+        r_times_h_n(z_)
+        z_times_h(z_)
+        sum_n(z_)
+        tanh_n(z_)
+        z_minus_1_times_n(y)
+        blend_and_store(y)
+        z_minus_1_times_n(z_)
+        blend_and_store(z_)

@@ -65,12 +65,14 @@ def tile_unitwisegru_pa_kernel(tc, x, h, w_ir, w_iz, w_in, w_hr, w_hz, w_hn, out
 
         for u in range(UNITS + 2):
             load_input_weight(u, R)
-            load_input_weight(u, N)
-            if u % 2 == 0 and u < UNITS:
-                load_pair(u // 2)
+            if u == 0:
+                load_pair(0)
             load_input_weight(u, Z)
+            load_input_weight(u, N)
             load_hidden_weight(u - 1, Z)
             load_hidden_weight(u - 1, R)
+            if u % 2 == 1 and u + 1 < UNITS:
+                load_pair((u + 1) // 2)
             load_hidden_weight(u - 2, N)
 
         ident_bf16 = keep.tile([P, P], BF16)
@@ -135,8 +137,8 @@ def tile_unitwisegru_pa_kernel(tc, x, h, w_ir, w_iz, w_in, w_hr, w_hz, w_hn, out
         w_codes = [keep.tile([P, GATES * HID], U32, align_bytes=64, name="w_codes%d" % u) for u in range(UNITS)]
         w_scales = [keep.tile([P, GATES * HID], U8, align_bytes=64, name="w_scales%d" % u) for u in range(UNITS)]
 
-        def z_on_vector(u):
-            return u in (0,1,2,4,6)
+        def n_on_vector(u):
+            return u < 4 or u == 5
 
         def regroup(u, g):
             if not is_unit(u):
@@ -150,7 +152,7 @@ def tile_unitwisegru_pa_kernel(tc, x, h, w_ir, w_iz, w_in, w_hr, w_hz, w_hn, out
                 whole = grouped_rz[u][:, g]
             src = wi_raw[u][:, g].rearrange("p t (c i) -> p c t i", i=RUN)
             dst = whole.rearrange("p (c i) t -> p c t i", i=RUN)
-            if g == N or (g == Z and z_on_vector(u)):
+            if g == Z or (g == N and n_on_vector(u)):
                 nc.vector.tensor_copy(out=dst, in_=src)
             else:
                 nc.scalar.copy(out=dst, in_=src)
@@ -305,69 +307,66 @@ def tile_unitwisegru_pa_kernel(tc, x, h, w_ir, w_iz, w_in, w_hr, w_hz, w_hn, out
             nc.sync.dma_start(out=out[:, u, :], in_=result[:])
 
         def step(a):
-            regroup(a, R)
-            r_times_h_n(a - 3)
-            sigmoid_z(a - 2)
-            quantise_n(a - 1)
-            sum_n(a - 3)
-            tanh_n(a - 3)
-            quantise_x(a - 1)
-            quantise_rz(a - 1)
             x_products_rz(a - 1)
-            h_product_z(a - 1)
             sum_r(a - 2)
+            r_times_h_n(a - 3)
+            z_times_h(a - 3)
+            sum_n(a - 3)
             sigmoid_r(a - 2)
+            sigmoid_z(a - 2)
+            tanh_n(a - 3)
+            h_product_z(a - 1)
             h_product_r(a - 1)
             h_product_n(a - 2)
             x_product_n(a - 2)
-            regroup(a, N)
-            z_minus_1_times_n(a - 3)
-            fetch_h(a)
-            fetch_x(a)
+            transpose_pair(a + 1)
             fetch_x_rz(a - 1)
             add_x_z(a - 1)
-            if not z_on_vector(a):
-                regroup(a, Z)
-            transpose_pair(a + 1)
-            if z_on_vector(a):
-                regroup(a, Z)
-            z_times_h(a - 2)
+            regroup(a, Z)
+            regroup(a + 1, R)
+            fetch_h(a + 1)
+            fetch_x(a + 1)
+            quantise_n(a - 1)
+            regroup(a, N)
+            quantise_x(a)
+            z_minus_1_times_n(a - 3)
+            quantise_rz(a)
             blend_and_store(a - 3)
 
         for a in range(-1, UNITS):
             step(a)
         y, z_ = UNITS - 2, UNITS - 1
-        h_product_z(z_)
-        r_times_h_n(y - 1)
-        sigmoid_z(y)
-        quantise_n(z_)
-        sum_n(y - 1)
-        tanh_n(y - 1)
-        quantise_rz(z_)
         x_products_rz(z_)
-        sum_r(y)
-        sigmoid_r(y)
-        h_product_r(z_)
         h_product_n(y)
         x_product_n(y)
+        sum_r(y)
+        r_times_h_n(y - 1)
+        z_times_h(y - 1)
+        sum_n(y - 1)
+        sigmoid_r(y)
+        tanh_n(y - 1)
+        h_product_z(z_)
+        h_product_r(z_)
         h_product_n(z_)
-        x_product_n(z_)
         fetch_x_rz(z_)
         add_x_z(z_)
-        z_times_h(y)
-        z_minus_1_times_n(y - 1)
-        blend_and_store(y - 1)
+        sigmoid_z(y)
+        quantise_n(z_)
+        x_product_n(z_)
         r_times_h_n(y)
-        sum_r(z_)
-        sigmoid_r(z_)
+        z_minus_1_times_n(y - 1)
         sum_n(y)
-        sigmoid_z(z_)
+        sum_r(z_)
         tanh_n(y)
+        sigmoid_r(z_)
+        sigmoid_z(z_)
+        blend_and_store(y - 1)
+        z_times_h(y)
         r_times_h_n(z_)
-        z_times_h(z_)
+        z_minus_1_times_n(y)
         sum_n(z_)
         tanh_n(z_)
-        z_minus_1_times_n(y)
         blend_and_store(y)
+        z_times_h(z_)
         z_minus_1_times_n(z_)
         blend_and_store(z_)

@@ -44,7 +44,7 @@ def tile_unitwisegru_pa_kernel(tc, x, h, w_ir, w_iz, w_in, w_hr, w_hz, w_hn, out
         x_sb = [keep.tile([P, 2 * IN], BF16, name="x_sb%d" % k) for k in range(PAIRS)]
         h_sb = [keep.tile([P, 2, HID], BF16, name="h_sb%d" % k) for k in range(PAIRS)]
         wi_raw = [keep.tile([P, GATES, PACK, HID], BF16, name="wi_raw%d" % u) for u in range(UNITS)]
-        wh_sb = [keep.tile([P, GATES, H_ROWS, HID], BF16, name="wh_sb%d" % u) for u in range(UNITS)]
+        wh_sb = [keep.tile([P, GATES, 2, H_ROWS, HID], BF16, name="wh_sb%d" % k) for k in range(PAIRS)]
 
         def load_pair(k):
             units = slice(2 * k, 2 * k + 2)
@@ -60,7 +60,15 @@ def tile_unitwisegru_pa_kernel(tc, x, h, w_ir, w_iz, w_in, w_hr, w_hz, w_hn, out
         def load_hidden_weight(u, g):
             if 0 <= u < UNITS:
                 nc.sync.dma_start(
-                    out=wh_sb[u][:, g], in_=w_h[g][u].rearrange("(p c) o -> p c o", c=H_ROWS)
+                    out=wh_sb[u // 2][:, g, u % 2], in_=w_h[g][u].rearrange("(p c) o -> p c o", c=H_ROWS)
+                )
+
+        def load_hidden_pair(k, g):
+            if 0 <= k < PAIRS:
+                units = slice(2 * k, 2 * k + 2)
+                nc.sync.dma_start(
+                    out=wh_sb[k][:, g].rearrange("p u c o -> p u (c o)"),
+                    in_=w_h[g][units].rearrange("u (p c) o -> p u (c o)", c=H_ROWS),
                 )
 
         for u in range(UNITS + 2):
@@ -69,11 +77,13 @@ def tile_unitwisegru_pa_kernel(tc, x, h, w_ir, w_iz, w_in, w_hr, w_hz, w_hn, out
                 load_pair(0)
             load_input_weight(u, Z)
             load_input_weight(u, N)
-            load_hidden_weight(u - 1, Z)
-            load_hidden_weight(u - 1, R)
+            if u % 2 == 1:
+                load_hidden_pair((u - 1) // 2, Z)
+                load_hidden_pair((u - 1) // 2, R)
             if u % 2 == 1 and u + 1 < UNITS:
                 load_pair((u + 1) // 2)
-            load_hidden_weight(u - 2, N)
+            if u % 2 == 0:
+                load_hidden_pair((u - 2) // 2, N)
 
         ident_bf16 = keep.tile([P, P], BF16)
         make_identity(nc, ident_bf16[:])
@@ -190,7 +200,7 @@ def tile_unitwisegru_pa_kernel(tc, x, h, w_ir, w_iz, w_in, w_hr, w_hz, w_hn, out
                 nc.tensor.matmul(
                     out=acc,
                     lhsT=hT[u // 2][:, u % 2, c, :],
-                    rhs=wh_sb[u][:, g, c, :],
+                    rhs=wh_sb[u // 2][:, g, u % 2, c, :],
                     start=(c == 0),
                     stop=(stop and c == H_ROWS - 1),
                 )

@@ -148,7 +148,7 @@ def tile_unitwisegru_pa_kernel(tc, x, h, w_ir, w_iz, w_in, w_hr, w_hz, w_hn, out
         w_scales = [keep.tile([P, GATES * HID], U8, align_bytes=64, name="w_scales%d" % u) for u in range(UNITS)]
 
         def n_on_vector(u):
-            return u < 4 or u == 5
+            return u not in (4, 7)
 
         def regroup(u, g):
             if not is_unit(u):
@@ -318,30 +318,30 @@ def tile_unitwisegru_pa_kernel(tc, x, h, w_ir, w_iz, w_in, w_hr, w_hz, w_hn, out
 
         def step(a):
             x_products_rz(a - 1)
-            sum_r(a - 2)
             r_times_h_n(a - 3)
-            z_times_h(a - 3)
+            sum_r(a - 2)
             sum_n(a - 3)
-            sigmoid_r(a - 2)
-            sigmoid_z(a - 2)
-            tanh_n(a - 3)
-            h_product_z(a - 1)
-            h_product_r(a - 1)
+            z_times_h(a - 3)
+            blend_and_store(a - 4)
             h_product_n(a - 2)
             x_product_n(a - 2)
-            transpose_pair(a + 1)
+            h_product_z(a - 1)
+            h_product_r(a - 1)
+            sigmoid_r(a - 2)
+            tanh_n(a - 3)
             fetch_x_rz(a - 1)
-            add_x_z(a - 1)
+            sigmoid_z(a - 2)
             regroup(a, Z)
+            transpose_pair(a + 1)
+            regroup(a, N)
+            quantise_n(a - 1)
+            add_x_z(a - 1)
             regroup(a + 1, R)
+            quantise_rz(a)
             fetch_h(a + 1)
             fetch_x(a + 1)
-            quantise_n(a - 1)
-            regroup(a, N)
             quantise_x(a)
             z_minus_1_times_n(a - 3)
-            quantise_rz(a)
-            blend_and_store(a - 3)
 
         for a in range(-1, UNITS):
             step(a)
@@ -349,14 +349,14 @@ def tile_unitwisegru_pa_kernel(tc, x, h, w_ir, w_iz, w_in, w_hr, w_hz, w_hn, out
         x_products_rz(z_)
         h_product_n(y)
         x_product_n(y)
-        sum_r(y)
         r_times_h_n(y - 1)
-        z_times_h(y - 1)
+        sum_r(y)
         sum_n(y - 1)
         sigmoid_r(y)
         tanh_n(y - 1)
-        h_product_z(z_)
+        blend_and_store(y - 2)
         h_product_r(z_)
+        h_product_z(z_)
         h_product_n(z_)
         fetch_x_rz(z_)
         add_x_z(z_)
@@ -364,11 +364,12 @@ def tile_unitwisegru_pa_kernel(tc, x, h, w_ir, w_iz, w_in, w_hr, w_hz, w_hn, out
         quantise_n(z_)
         x_product_n(z_)
         r_times_h_n(y)
+        z_times_h(y - 1)
         z_minus_1_times_n(y - 1)
-        sum_n(y)
         sum_r(z_)
-        tanh_n(y)
         sigmoid_r(z_)
+        sum_n(y)
+        tanh_n(y)
         sigmoid_z(z_)
         blend_and_store(y - 1)
         z_times_h(y)
@@ -376,7 +377,7 @@ def tile_unitwisegru_pa_kernel(tc, x, h, w_ir, w_iz, w_in, w_hr, w_hz, w_hn, out
         z_minus_1_times_n(y)
         sum_n(z_)
         tanh_n(z_)
-        blend_and_store(y)
         z_times_h(z_)
+        blend_and_store(y)
         z_minus_1_times_n(z_)
         blend_and_store(z_)

@@ -77,13 +77,16 @@ def tile_unitwisegru_pa_kernel(tc, x, h, w_ir, w_iz, w_in, w_hr, w_hz, w_hn, out
                 load_pair(0)
             load_input_weight(u, Z)
             load_input_weight(u, N)
-            if u % 2 == 1:
-                load_hidden_pair((u - 1) // 2, Z)
+            if u % 2 == 1 and u < 7:
                 load_hidden_pair((u - 1) // 2, R)
+                load_hidden_pair((u - 1) // 2, Z)
             if u % 2 == 1 and u + 1 < UNITS:
                 load_pair((u + 1) // 2)
-            if u % 2 == 0:
+            if u % 2 == 0 and u < 8:
                 load_hidden_pair((u - 2) // 2, N)
+            if u >= 8:
+                for g in (R, Z, N):
+                    load_hidden_weight(u - 2, g)
 
         ident_bf16 = keep.tile([P, P], BF16)
         make_identity(nc, ident_bf16[:])
@@ -313,43 +316,45 @@ def tile_unitwisegru_pa_kernel(tc, x, h, w_ir, w_iz, w_in, w_hr, w_hz, w_hn, out
             if not is_unit(u):
                 return
             result = keep.tile([P, HID], F32, name="result%d" % u)
-            nc.vector.tensor_tensor(out=result[:], in0=z_h[u][:], in1=z_n[u][:], op=ALU.subtract)
-            nc.sync.dma_start(out=out[:, u, :], in_=result[:])
+            for cols in column_parts(u):
+                nc.vector.tensor_tensor(out=result[:, cols], in0=z_h[u][:, cols], in1=z_n[u][:, cols], op=ALU.subtract)
+                nc.sync.dma_start(out=out[:, u, cols], in_=result[:, cols])
 
         def step(a):
             x_products_rz(a - 1)
             r_times_h_n(a - 3)
+            z_minus_1_times_n(a - 4)
             sum_r(a - 2)
             sum_n(a - 3)
             z_times_h(a - 3)
             blend_and_store(a - 4)
             h_product_n(a - 2)
             x_product_n(a - 2)
-            h_product_z(a - 1)
             h_product_r(a - 1)
+            h_product_z(a - 1)
             sigmoid_r(a - 2)
             tanh_n(a - 3)
             fetch_x_rz(a - 1)
             sigmoid_z(a - 2)
             regroup(a, Z)
             transpose_pair(a + 1)
-            regroup(a, N)
             quantise_n(a - 1)
+            regroup(a, N)
             add_x_z(a - 1)
             regroup(a + 1, R)
             quantise_rz(a)
             fetch_h(a + 1)
             fetch_x(a + 1)
             quantise_x(a)
-            z_minus_1_times_n(a - 3)
 
         for a in range(-1, UNITS):
             step(a)
         y, z_ = UNITS - 2, UNITS - 1
-        x_products_rz(z_)
         h_product_n(y)
         x_product_n(y)
+        x_products_rz(z_)
         r_times_h_n(y - 1)
+        z_minus_1_times_n(y - 2)
         sum_r(y)
         sum_n(y - 1)
         sigmoid_r(y)
@@ -374,9 +379,9 @@ def tile_unitwisegru_pa_kernel(tc, x, h, w_ir, w_iz, w_in, w_hr, w_hz, w_hn, out
         blend_and_store(y - 1)
         z_times_h(y)
         r_times_h_n(z_)
-        z_minus_1_times_n(y)
         sum_n(z_)
         tanh_n(z_)
+        z_minus_1_times_n(y)
         z_times_h(z_)
         blend_and_store(y)
         z_minus_1_times_n(z_)

from contextlib import ExitStack

import concourse.mybir as mybir
from concourse.masks import make_identity

BF16 = mybir.dt.bfloat16
F32 = mybir.dt.float32
U32 = mybir.dt.uint32
U8 = mybir.dt.uint8
FP8X4 = mybir.dt.float8_e4m3fn_x4
ACT = mybir.ActivationFunctionType
ALU = mybir.AluOpType

P = 128
UNITS = 8
PAIRS = UNITS // 2
IN = 512
HID = 256
PACK = 4
H_ROWS = HID // P
GATES = 3
R = 0
Z = 1
N = 2
RUN = 4
UNITS_WITH_Z_ON_VECTOR = 4

FLOPS = 2 * P * UNITS * GATES * (IN * HID + HID * HID)


def tile_unitwisegru_pa_kernel(tc, x, h, w_ir, w_iz, w_in, w_hr, w_hz, w_hn, out):
    nc = tc.nc
    w_i = (w_ir, w_iz, w_in)
    w_h = (w_hr, w_hz, w_hn)
    RZ_COLS = slice(0, 2 * HID)
    N_COLS = slice(2 * HID, 3 * HID)
    with ExitStack() as ctx:
        keep = ctx.enter_context(tc.tile_pool(name="keep", bufs=1))
        work = ctx.enter_context(tc.tile_pool(name="work", bufs=3))
        psum_t = ctx.enter_context(tc.psum_pool(name="psum_t", bufs=2))
        psum_g = ctx.enter_context(tc.psum_pool(name="psum_g", bufs=2))
        ctx.enter_context(tc.manual_schedule())

        x_sb = [keep.tile([P, 2 * IN], BF16, name="x_sb%d" % k) for k in range(PAIRS)]
        h_sb = [keep.tile([P, 2, HID], BF16, name="h_sb%d" % k) for k in range(PAIRS)]
        wi_raw = [keep.tile([P, GATES, PACK, HID], BF16, name="wi_raw%d" % u) for u in range(UNITS)]
        wh_sb = [keep.tile([P, GATES, 2, H_ROWS, HID], BF16, name="wh_sb%d" % k) for k in range(PAIRS)]

        def load_pair(k):
            units = slice(2 * k, 2 * k + 2)
            nc.sync.dma_start(out=h_sb[k][:], in_=h[:, units, :])
            nc.sync.dma_start(out=x_sb[k][:], in_=x[:, units, :].rearrange("b u i -> b (u i)"))

        def load_input_weight(u, g):
            if 0 <= u < UNITS:
                nc.sync.dma_start(
                    out=wi_raw[u][:, g], in_=w_i[g][u].rearrange("(p j) o -> p j o", j=PACK)
                )

        def load_hidden_weight(u, g):
            if 0 <= u < UNITS:
                nc.sync.dma_start(
                    out=wh_sb[u // 2][:, g, u % 2], in_=w_h[g][u].rearrange("(p c) o -> p c o", c=H_ROWS)
                )

        def load_hidden_pair(k, g):
            if 0 <= k < PAIRS:
                units = slice(2 * k, 2 * k + 2)
                nc.sync.dma_start(
                    out=wh_sb[k][:, g].rearrange("p u c o -> p u (c o)"),
                    in_=w_h[g][units].rearrange("u (p c) o -> p u (c o)", c=H_ROWS),
                )

        for u in range(UNITS + 2):
            load_input_weight(u, R)
            if u == 0:
                load_pair(0)
            load_input_weight(u, Z)
            load_input_weight(u, N)
            if u % 2 == 1 and u < 7:
                load_hidden_pair((u - 1) // 2, R)
                load_hidden_pair((u - 1) // 2, Z)
            if u % 2 == 1 and u + 1 < UNITS:
                load_pair((u + 1) // 2)
            if u % 2 == 0 and u < 8:
                load_hidden_pair((u - 2) // 2, N)
            if u >= 8:
                for g in (R, Z, N):
                    load_hidden_weight(u - 2, g)

        ident_bf16 = keep.tile([P, P], BF16)
        make_identity(nc, ident_bf16[:])
        ident_f32 = keep.tile([P, P], F32)
        make_identity(nc, ident_f32[:])
        warm = keep.tile([P, 1], F32)
        nc.vector.memset(warm[:], 0.0)
        nc.scalar.activation(out=warm[:], in_=warm[:], func=ACT.Sigmoid)

        def is_unit(u):
            return 0 <= u < UNITS

        def is_pair(twice_k):
            return twice_k % 2 == 0 and 0 <= twice_k // 2 < PAIRS

        transposed = {}
        hT = [keep.tile([P, 2, H_ROWS, P], BF16, name="hT%d" % k) for k in range(PAIRS)]
        x_grouped = {}
        x_codes = [keep.tile([P, 2 * P], U32, align_bytes=64, name="x_codes%d" % k) for k in range(PAIRS)]
        x_scales = [keep.tile([P, 2 * P], U8, align_bytes=64, name="x_scales%d" % k) for k in range(PAIRS)]

        def transpose_pair(twice_k):
            if not is_pair(twice_k):
                return
            k = twice_k // 2
            h_cols = h_sb[k][:].rearrange("b i (p c) -> b i c p", c=H_ROWS)
            ht = psum_t.tile([P, 2, H_ROWS, P], BF16, tag="transposed")
            for i in range(2):
                for c in range(H_ROWS):
                    nc.tensor.transpose(ht[:, i, c, :], h_cols[:, i, c, :], ident_bf16[:])
            x_words = x_sb[k][:].bitcast(F32).rearrange("b (i p s) -> b i s p", i=2, s=2)
            xt = psum_t.tile([P, 2, 2, P], F32, tag="transposed")
            for i in range(2):
                for s in range(2):
                    nc.tensor.transpose(xt[:, i, s, :], x_words[:, i, s, :], ident_f32[:])
            transposed[k] = (ht, xt)

        def fetch_h(twice_k):
            if is_pair(twice_k):
                k = twice_k // 2
                nc.scalar.copy(out=hT[k][:], in_=transposed[k][0][:])

        def fetch_x(twice_k):
            if not is_pair(twice_k):
                return
            k = twice_k // 2
            x_grouped[k] = work.tile([P, 2 * P * PACK], BF16, align_bytes=64, name="x_grouped")
            dst = x_grouped[k][:].bitcast(F32).rearrange("p (i b s) -> p i b s", i=2, s=2)
            nc.scalar.copy(out=dst, in_=transposed[k][1][:].rearrange("p i s b -> p i b s"))

        def quantise_x(twice_k):
            if not is_pair(twice_k):
                return
            k = twice_k // 2
            nc.vector.quantize_mx(
                out=x_codes[k][:].bitcast(FP8X4), scales=x_scales[k][:], in_=x_grouped[k][:]
            )

        grouped_rz = {}
        grouped_n = {}
        w_codes = [keep.tile([P, GATES * HID], U32, align_bytes=64, name="w_codes%d" % u) for u in range(UNITS)]
        w_scales = [keep.tile([P, GATES * HID], U8, align_bytes=64, name="w_scales%d" % u) for u in range(UNITS)]

        def n_on_vector(u):
            return u not in (4, 7)

        def regroup(u, g):
            if not is_unit(u):
                return
            if g == N:
                grouped_n[u] = work.tile([P, HID, PACK], BF16, align_bytes=64, name="grouped_n")
                whole = grouped_n[u][:]
            else:
                if u not in grouped_rz:
                    grouped_rz[u] = work.tile([P, 2, HID, PACK], BF16, align_bytes=64, name="grouped_rz")
                whole = grouped_rz[u][:, g]
            src = wi_raw[u][:, g].rearrange("p t (c i) -> p c t i", i=RUN)
            dst = whole.rearrange("p (c i) t -> p c t i", i=RUN)
            if g == Z or (g == N and n_on_vector(u)):
                nc.vector.tensor_copy(out=dst, in_=src)
            else:
                nc.scalar.copy(out=dst, in_=src)

        def quantise_rz(u):
            if is_unit(u):
                nc.vector.quantize_mx(
                    out=w_codes[u][:, RZ_COLS].bitcast(FP8X4),
                    scales=w_scales[u][:, RZ_COLS],
                    in_=grouped_rz[u][:].rearrange("p g o t -> p (g o t)"),
                )

        def quantise_n(u):
            if is_unit(u):
                nc.vector.quantize_mx(
                    out=w_codes[u][:, N_COLS].bitcast(FP8X4),
                    scales=w_scales[u][:, N_COLS],
                    in_=grouped_n[u][:].rearrange("p o t -> p (o t)"),
                )

        def matmul_x(u, acc, cols):
            b_cols = slice((u % 2) * P, (u % 2 + 1) * P)
            nc.tensor.matmul_mx(
                out=acc,
                lhsT=x_codes[u // 2][:, b_cols].bitcast(FP8X4),
                lhsT_scale=x_scales[u // 2][:, b_cols],
                rhs=w_codes[u][:, cols].bitcast(FP8X4),
                rhs_scale=w_scales[u][:, cols],
                start=True,
                stop=True,
            )

        def matmul_h(u, g, acc, stop=True):
            for c in range(H_ROWS):
                nc.tensor.matmul(
                    out=acc,
                    lhsT=hT[u // 2][:, u % 2, c, :],
                    rhs=wh_sb[u // 2][:, g, u % 2, c, :],
                    start=(c == 0),
                    stop=(stop and c == H_ROWS - 1),
                )

        x_rz = {}
        x_rz_sb = {}
        h_r = {}
        z_sum = {}
        xh_n = {}
        r_sum = {}
        r = {}
        z = {}
        rh_n = {}
        n_sum = {}
        z_h = {}
        n_gate = {}
        z_n = {}

        def x_products_rz(u):
            if is_unit(u):
                x_rz[u] = psum_g.tile([P, 2 * HID], F32, name="x_rz", bufs=1)
                matmul_x(u, x_rz[u][:], RZ_COLS)

        def fetch_x_rz(u):
            if is_unit(u):
                x_rz_sb[u] = work.tile([P, 2, HID], F32, name="x_rz_sb")
                nc.scalar.copy(out=x_rz_sb[u][:], in_=x_rz[u][:].rearrange("p (g o) -> p g o", g=2))

        def h_product_r(u):
            if is_unit(u):
                h_r[u] = psum_g.tile([P, HID], F32, name="h_r", bufs=1)
                matmul_h(u, R, h_r[u][:])

        def h_product_z(u):
            if is_unit(u):
                z_sum[u] = psum_g.tile([P, HID], F32, name="z_sum")
                matmul_h(u, Z, z_sum[u][:], stop=False)

        def add_x_z(u):
            if is_unit(u):
                nc.tensor.matmul(
                    out=z_sum[u][:], lhsT=ident_f32[:], rhs=x_rz_sb[u][:, Z, :], start=False, stop=True
                )

        def h_product_n(u):
            if is_unit(u):
                xh_n[u] = psum_g.tile([P, 2, HID], F32, name="xh_n")
                matmul_h(u, N, xh_n[u][:, 1, :])

        def x_product_n(u):
            if is_unit(u):
                matmul_x(u, xh_n[u][:, 0, :], N_COLS)

        def column_parts(u):
            if u == UNITS - 1:
                return (slice(0, HID // 2), slice(HID // 2, HID))
            return (slice(0, HID),)

        def sum_r(u):
            if is_unit(u):
                r_sum[u] = work.tile([P, HID], F32, name="r_sum")
                for cols in column_parts(u):
                    nc.vector.tensor_tensor(out=r_sum[u][:, cols], in0=h_r[u][:, cols], in1=x_rz_sb[u][:, R, cols], op=ALU.add)

        def sigmoid_r(u):
            if is_unit(u):
                r[u] = work.tile([P, HID], F32, name="r")
                for cols in column_parts(u):
                    nc.scalar.activation(out=r[u][:, cols], in_=r_sum[u][:, cols], func=ACT.Sigmoid)

        def sigmoid_z(u):
            if is_unit(u):
                z[u] = work.tile([P, HID], F32, name="z")
                nc.scalar.activation(out=z[u][:], in_=z_sum[u][:], func=ACT.Sigmoid)

        def r_times_h_n(u):
            if is_unit(u):
                rh_n[u] = work.tile([P, HID], F32, name="rh_n")
                for cols in column_parts(u):
                    nc.vector.tensor_tensor(out=rh_n[u][:, cols], in0=xh_n[u][:, 1, cols], in1=r[u][:, cols], op=ALU.mult)

        def z_times_h(u):
            if is_unit(u):
                z_h[u] = work.tile([P, HID], F32, name="z_h")
                nc.vector.tensor_tensor(out=z_h[u][:], in0=h_sb[u // 2][:, u % 2, :], in1=z[u][:], op=ALU.mult)

        def sum_n(u):
            if is_unit(u):
                n_sum[u] = work.tile([P, HID], F32, name="n_sum")
                for cols in column_parts(u):
                    nc.vector.tensor_tensor(out=n_sum[u][:, cols], in0=xh_n[u][:, 0, cols], in1=rh_n[u][:, cols], op=ALU.add)

        def tanh_n(u):
            if not is_unit(u):
                return
            n_gate[u] = work.tile([P, HID], F32, name="n_gate")
            for cols in column_parts(u):
                nc.scalar.activation(out=n_gate[u][:, cols], in_=n_sum[u][:, cols], func=ACT.Tanh)

        def z_minus_1_times_n(u):
            if not is_unit(u):
                return
            z_n[u] = work.tile([P, HID], F32, name="z_n")
            for cols in column_parts(u):
                nc.vector.scalar_tensor_tensor(
                    out=z_n[u][:, cols], in0=z[u][:, cols], scalar=1.0, in1=n_gate[u][:, cols], op0=ALU.subtract, op1=ALU.mult
                )

        def blend_and_store(u):
            if not is_unit(u):
                return
            result = keep.tile([P, HID], F32, name="result%d" % u)
            for cols in column_parts(u):
                nc.vector.tensor_tensor(out=result[:, cols], in0=z_h[u][:, cols], in1=z_n[u][:, cols], op=ALU.subtract)
                nc.sync.dma_start(out=out[:, u, cols], in_=result[:, cols])

        def step(a):
            x_products_rz(a - 1)
            r_times_h_n(a - 3)
            z_minus_1_times_n(a - 4)
            sum_r(a - 2)
            sum_n(a - 3)
            z_times_h(a - 3)
            blend_and_store(a - 4)
            h_product_n(a - 2)
            x_product_n(a - 2)
            h_product_r(a - 1)
            h_product_z(a - 1)
            sigmoid_r(a - 2)
            tanh_n(a - 3)
            fetch_x_rz(a - 1)
            sigmoid_z(a - 2)
            regroup(a, Z)
            transpose_pair(a + 1)
            quantise_n(a - 1)
            regroup(a, N)
            add_x_z(a - 1)
            regroup(a + 1, R)
            quantise_rz(a)
            fetch_h(a + 1)
            fetch_x(a + 1)
            quantise_x(a)

        for a in range(-1, UNITS):
            step(a)
        y, z_ = UNITS - 2, UNITS - 1
        h_product_n(y)
        x_product_n(y)
        x_products_rz(z_)
        r_times_h_n(y - 1)
        z_minus_1_times_n(y - 2)
        sum_r(y)
        sum_n(y - 1)
        sigmoid_r(y)
        tanh_n(y - 1)
        blend_and_store(y - 2)
        h_product_r(z_)
        h_product_z(z_)
        h_product_n(z_)
        fetch_x_rz(z_)
        add_x_z(z_)
        sigmoid_z(y)
        quantise_n(z_)
        x_product_n(z_)
        r_times_h_n(y)
        z_times_h(y - 1)
        z_minus_1_times_n(y - 1)
        sum_r(z_)
        sigmoid_r(z_)
        sum_n(y)
        tanh_n(y)
        sigmoid_z(z_)
        blend_and_store(y - 1)
        z_times_h(y)
        r_times_h_n(z_)
        sum_n(z_)
        tanh_n(z_)
        z_minus_1_times_n(y)
        z_times_h(z_)
        blend_and_store(y)
        z_minus_1_times_n(z_)
        blend_and_store(z_)
